import numpy as np
import ml_dtypes


def mxq(x, axis, fmt="e4m3"):
    dtype, down = {"e4m3": (ml_dtypes.float8_e4m3fn, 7), "e5m2": (ml_dtypes.float8_e5m2, 14)}[fmt]
    v = np.moveaxis(np.asarray(x, np.float32).astype(ml_dtypes.bfloat16).astype(np.float64), axis, -1)
    blocks = v.reshape(v.shape[:-1] + (-1, 32))
    amax = np.abs(blocks).max(-1, keepdims=True)
    byte = np.maximum(np.where(amax > 0, np.frexp(amax)[1] - 1 + 127, 0) - down, 1)
    scale = np.exp2(byte - 127.0)
    codes = (blocks / scale).astype(np.float32).astype(dtype).astype(np.float64)
    return np.moveaxis((codes * scale).reshape(v.shape), -1, axis)


WIDE = False


def mx_kscale(k):
    if not WIDE:
        return np.ones(k)
    levels = np.array([18, -18])
    if k % 512:
        return np.exp2(np.random.permutation(np.resize(levels, k // 32))).repeat(32)
    a = np.empty((k // 512, 16))
    for p in range(k // 512):
        a[p, :8] = np.random.permutation(np.resize(levels, 8))
        for g in range(8):
            far = levels[np.abs(levels - a[p, g]) >= 10]
            a[p, g + 8] = far[np.random.randint(len(far))]
    return np.exp2(a.ravel()).repeat(32)


BF16 = ml_dtypes.bfloat16


def bf(x):
    return np.asarray(x, np.float32).astype(BF16)


def f64(x):
    return np.asarray(x).astype(np.float64)


B, NT, N, C, DV, TM = 2, 128, 512, 1024, 1024, 128


def softmax(s):
    e = np.exp(s - s.max(-1, keepdims=True))
    return e / e.sum(-1, keepdims=True)


def votes(q, k, ki):
    scale = C ** -0.5
    aw = softmax(f64(q) @ f64(k).transpose(0, 2, 1) * scale)
    awi = softmax(f64(q) @ f64(ki).transpose(0, 2, 1) * scale)
    D = aw - awi
    ones_cnt = np.where(D > 0, 1.0, 0.0).sum(axis=1)
    half_cnt = np.where(D == 0, 1.0, 0.0).sum(axis=1)
    return ones_cnt / NT, half_cnt / NT


def setup_inputs():
    s = mx_kscale(B * N).reshape(B, N, 1)
    u = mx_kscale(DV)
    q = bf(np.random.standard_normal((B, 1, C)) + np.random.standard_normal((B, NT, C)))
    k = bf(np.random.standard_normal((B, N, C)) * 1.4)
    ki = bf(np.random.standard_normal((B, N, C)) * 1.4)
    ki[-1] = k[-1]
    xs0 = bf(np.random.standard_normal((B, N, C)))
    xis0 = bf(np.random.standard_normal((B, N, C)))
    Wv0 = bf(np.random.standard_normal((C, DV)) * 1.8 / np.sqrt(C))
    g = bf(np.random.standard_normal((B, N, DV)) * np.exp2(np.random.randint(-6, 1, (B, N, 1))) * 2.0 / s * u)
    rgb_ratio, eq_ratio = votes(q, k, ki)
    return {'q': q, 'k': k, 'ki': ki,
            'xs': bf(f64(xs0) * s),
            'xis': bf(f64(xis0) * s),
            'Wv': bf(f64(Wv0) / u),
            'rgb_ratio': np.asarray(rgb_ratio, np.float32),
            'eq_ratio': np.asarray(eq_ratio, np.float32),
            'grad_out': g}


def reference(q, k, ki, xs, xis, Wv, rgb_ratio, eq_ratio, grad_out):
    g = f64(grad_out).reshape(B * N, DV)
    rgb = f64(rgb_ratio).reshape(B * N, 1)
    eq = f64(eq_ratio).reshape(B * N, 1)
    tir = 1.0 - rgb - eq
    dv = g * (rgb + eq)
    dvi = g * (tir + eq)
    dxs = mxq(dv, 1, 'e5m2') @ mxq(f64(Wv), 1, 'e4m3').T
    x2 = np.concatenate([f64(xs).reshape(B * N, C), f64(xis).reshape(B * N, C)], axis=0)
    dz2 = np.concatenate([dv, dvi], axis=0)
    dWv = mxq(x2, 0, 'e4m3').T @ mxq(dz2, 0, 'e5m2')
    return dxs.reshape(B, N, C), dWv

@@ -1,0 +1,430 @@
+from contextlib import ExitStack
+
+import concourse.mybir as mybir
+from concourse.masks import make_identity
+
+B, N, C, DV = 2, 512, 1024, 1024
+FLOPS = 2 * B * N * C * DV * 3
+BYTES = 2 * (3 * B * N * C + C * DV) + 8 * B * N + 4 * (B * N * C + C * DV)
+
+F32 = mybir.dt.float32
+BF16 = mybir.dt.bfloat16
+U32 = mybir.dt.uint32
+U8 = mybir.dt.uint8
+E4 = mybir.dt.float8_e4m3fn_x4
+E5 = mybir.dt.float8_e5m2_x4
+ALU = mybir.AluOpType
+
+P = 128
+PACK = 4
+HALF = 512
+ROWS = C // P
+SCALAR_X = ((1, 0), (1, 1), (1, 2))
+SPOS = (0, 0, 4)
+VE = (9, 11, 13, 15)
+WARM = (3, 0)
+
+
+def tile_crossattention_for_fusion_temporal_pa_v_kernel(
+    tc, q, k, ki, xs, xis, Wv, rgb_ratio, eq_ratio, grad_out, out_0, out_1
+):
+    nc = tc.nc
+    with ExitStack() as ctx:
+        keep = ctx.enter_context(tc.tile_pool(name="keep", bufs=1))
+        psum = ctx.enter_context(tc.psum_pool(name="psum", bufs=1))
+        ctx.enter_context(tc.manual_schedule())
+
+        def sbuf(name, width, dtype):
+            return keep.tile([P, width], dtype, name=name, align_bytes=64)
+
+        queues = {"sync": [], "vector": [], "scalar": [], "tensor": []}
+        tiles = {}
+        slot_free = {}
+
+        def step(engine, key, needs, emit):
+            queues[engine].append((key, list(needs), emit))
+
+        def reuse(slot, release_key):
+            before = slot_free.get(slot)
+            slot_free[slot] = release_key
+            return [] if before is None else [before]
+
+        ident = sbuf("ident", P, F32)
+        make_identity(nc, ident[:])
+
+        rgb = keep.tile([P, B, PACK], F32, name="rgb")
+        eq = keep.tile([P, B, PACK], F32, name="eq")
+        gates = [keep.tile([P, B, PACK], F32, name="gate%d" % s) for s in range(2)]
+        w_raw = {(ch, rp): keep.tile([P, 2, DV], BF16, name="w%d%d" % (ch, rp)) for ch in range(2) for rp in range(2)}
+        g_raw = {(b, jp): keep.tile([P, 2, DV], BF16, name="g%d%d" % (b, jp)) for b in range(B) for jp in range(2)}
+        x_raw = keep.tile([P, 4, PACK, C], BF16, name="x")
+        dz = {(t, h): sbuf("dz%d%d" % (t, h), PACK * HALF, BF16) for t in range(4) for h in range(2)}
+        codes = {}
+        scales = {}
+        names = ([("w", ch, h) for ch in range(2) for h in range(2)] + [("dvt", b, h) for b in range(B) for h in range(2)]
+                 + [("dz", t, h) for t in range(4) for h in range(2)] + [("x", s, rp) for s in range(2) for rp in range(4)])
+        for name in names:
+            label = "_".join(str(part) for part in name)
+            codes[name] = sbuf("c_" + label, HALF, U32)
+            scales[name] = sbuf("s_" + label, HALF, U8)
+
+        def load(key, dst, src):
+            step("sync", key, [], lambda: nc.sync.dma_start(out=dst, in_=src))
+
+        nc.scalar.dma_start(out=rgb[:], in_=rgb_ratio.rearrange("b (p j) -> p b j", j=PACK))
+        nc.scalar.dma_start(out=eq[:], in_=eq_ratio.rearrange("b (p j) -> p b j", j=PACK))
+        w_view = Wv.rearrange("(ch r p) d -> ch p r d", ch=2, p=P)
+        def load_w(ch, rp):
+            load(("load_w", ch, rp), w_raw[ch, rp][:], w_view[ch][:, 2 * rp:2 * rp + 2, :])
+
+        def load_g(b, jp):
+            load(("load_g", b, jp), g_raw[b, jp][:],
+                 grad_out[b].rearrange("(p j) d -> p j d", j=PACK)[:, 2 * jp:2 * jp + 2, :])
+
+        load_g(0, 0)
+        load_g(0, 1)
+        load_w(0, 0)
+        load_w(0, 1)
+        load_w(1, 0)
+        load_w(1, 1)
+        load_g(1, 0)
+        load_g(1, 1)
+        for t, src in enumerate([xs[0], xs[1], xis[0], xis[1]]):
+            load(("load_x", t), x_raw[:, t], src.rearrange("(p j) c -> p j c", j=PACK))
+
+        def make_gates():
+            nc.vector.tensor_tensor(out=gates[0][:], in0=rgb[:], in1=eq[:], op=ALU.add)
+            nc.vector.tensor_scalar(out=gates[1][:], in0=rgb[:], scalar1=-1.0, scalar2=1.0, op0=ALU.mult, op1=ALU.add)
+
+        def gate(stream, b, jp, halves=(0, 1)):
+            for h in halves:
+                def emit(h=h):
+                    for i in range(2):
+                        j = 2 * jp + i
+                        nc.vector.tensor_scalar(
+                            out=dz[2 * stream + b, h][:, j * HALF:(j + 1) * HALF].rearrange("p (u w e) -> p u w e", u=2, e=2),
+                            in0=g_raw[b, jp][:, i, h * HALF:(h + 1) * HALF].rearrange("p (w u e) -> p u w e", u=2, e=2),
+                            scalar1=gates[stream][:, b, j:j + 1], scalar2=None, op0=ALU.mult)
+
+                step("vector", ("gated", 2 * stream + b, h, jp), [("load_g", b, jp)], emit)
+
+        counts = {"vector": 0, "scalar": 0, "t": 0, "r1": 0}
+
+        def interleave(engine, name):
+            slot = "grp_%s%d" % (engine, counts[engine] % 3)
+            counts[engine] = counts[engine] + 1
+            needs = reuse(slot, ("quantised",) + name)
+            if name[0] == "dz":
+                t, h = name[1:]
+                needs = needs + [("gated", t, h, jp) for jp in range(2)]
+            else:
+                needs = needs + [("load_x", 2 * name[1] + b) for b in range(B)]
+
+            def emit():
+                grouped = sbuf(slot, PACK * HALF, BF16)
+                tiles[("grouped",) + name] = grouped
+                if name[0] == "dz":
+                    src = dz[t, h][:].rearrange("p (j c i) -> p c j i", j=PACK, i=4)
+                    dst = grouped[:].rearrange("p (c i j) -> p c j i", j=PACK, i=4)
+                else:
+                    s, rp = name[1:]
+                    src = x_raw[:, 2 * s:2 * s + 2, :, rp * 2 * P:(rp + 1) * 2 * P].rearrange("p b j (c i) -> p b c j i", i=4)
+                    dst = grouped[:].rearrange("p (b c i j) -> p b c j i", b=B, j=PACK, i=4)
+                if engine == "vector":
+                    nc.vector.tensor_copy(out=dst, in_=src)
+                else:
+                    nc.scalar.copy(out=dst, in_=src)
+
+            step(engine, ("grouped",) + name, needs, emit)
+
+        def quantise(name):
+            fmt = E5 if name[0] in ("dz", "dvt") else E4
+            if name[0] in ("w", "dvt"):
+                needs = [("copied",) + name + (pair,) for pair in range(2)]
+            else:
+                needs = [("grouped",) + name]
+
+            def emit():
+                nc.vector.quantize_mx(out=codes[name][:].bitcast(fmt), scales=scales[name][:],
+                                      in_=tiles[("grouped",) + name][:])
+
+            step("vector", ("quantised",) + name, needs, emit)
+
+        def transpose(name, pair, bank):
+            key = ("transposed",) + name + (pair,)
+            needs = reuse("bank%d" % bank, ("copied",) + name + (pair,))
+            if name[0] == "w":
+                ch, h = name[1:]
+                needs = needs + [("load_w", ch, pair)]
+            else:
+                b, jp = name[1:]
+                needs = needs + [("gated", b, pair, jp)]
+
+            def emit():
+                acc = psum.tile([P, 2, 2, P], F32, name="bank%d" % bank)
+                tiles[key] = acc
+                for i in range(2):
+                    for u in range(2):
+                        if name[0] == "w":
+                            row = w_raw[ch, pair][:, i, h * HALF:(h + 1) * HALF]
+                            words = row.bitcast(F32)[:, u::2]
+                        else:
+                            first = (2 * (2 * jp + i) + u) * P
+                            words = dz[b, pair][:].bitcast(F32)[:, first:first + P]
+                        nc.tensor.transpose(acc[:, i, u, :], words, ident[:])
+
+            step("tensor", key, needs, emit)
+
+        def copy_transposed(name, pair):
+            needs = [("transposed",) + name + (pair,)]
+            if pair == 0:
+                slot = "grp_t%d" % (counts["t"] % 4)
+                counts["t"] = counts["t"] + 1
+                needs = needs + reuse(slot, ("quantised",) + name)
+
+            def emit():
+                if pair == 0:
+                    tiles[("grouped",) + name] = sbuf(slot, PACK * HALF, BF16)
+                words = tiles[("grouped",) + name][:].bitcast(F32)[:, pair * HALF:(pair + 1) * HALF]
+                nc.scalar.copy(out=words.rearrange("p (i n u) -> p i n u", i=2, u=2),
+                               in_=tiles[("transposed",) + name + (pair,)][:].rearrange("p i u n -> p i n u"))
+
+            step("scalar", ("copied",) + name + (pair,), needs, emit)
+
+        def multiply(group, passes, bank=None):
+            last = 1 if group[0] == "out0" else 3
+            needs = []
+            if passes[0] == 0:
+                needs = reuse("bank%d" % bank, ("emptied",) + group)
+            operands = []
+            for t in passes:
+                if group[0] == "out0":
+                    b, j, ch = group[1:]
+                    operands.append((("dvt", b, j // 2), 2 * t + j % 2, E5, ("w", ch, t), E4))
+                else:
+                    r, h = group[1:]
+                    operands.append((("x", t // 2, r // 2), 2 * (t % 2) + r % 2, E4, ("dz", t, h), E5))
+            needs = needs + [("quantised",) + o[0] for o in operands] + [("quantised",) + o[3] for o in operands]
+
+            def emit():
+                if passes[0] == 0:
+                    tiles[group] = psum.tile([P, HALF], F32, name="bank%d" % bank)
+                for t, (fixed, block, fixed_fmt, moving, moving_fmt) in zip(passes, operands):
+                    cols = slice(block * P, (block + 1) * P)
+                    nc.tensor.matmul_mx(
+                        out=tiles[group][:],
+                        lhsT=codes[fixed][:, cols].bitcast(fixed_fmt), lhsT_scale=scales[fixed][:, cols],
+                        rhs=codes[moving][:].bitcast(moving_fmt), rhs_scale=scales[moving][:],
+                        start=(t == 0), stop=(t == last))
+
+            step("tensor", ("summed",) + group + (passes[-1],), needs, emit)
+
+        def empty(group, engine="scalar"):
+            last = 1 if group[0] == "out0" else 3
+            needs = [("summed",) + group + (last,)]
+            if group[0] == "out1":
+                slot = "res1_%d" % (counts["r1"] % 8)
+                counts["r1"] = counts["r1"] + 1
+                needs = needs + reuse(slot, ("stored",) + group)
+            elif group[1] == 1:
+                needs = needs + [("transposed", "w", group[2] // 2, h, group[2] % 2) for h in range(2)]
+
+            def emit():
+                if group[0] == "out0":
+                    b, j, ch = group[1:]
+                    if ch == 0:
+                        tiles["res0", b, j] = keep.tile([P, C], F32, name="res0_%d" % j if b == 0 else "w%d%d" % (j // 2, j % 2))
+                    dst = tiles["res0", b, j][:, ch * HALF:(ch + 1) * HALF]
+                    src = tiles[group][:]
+                else:
+                    tiles[("res",) + group] = sbuf(slot, HALF, F32)
+                    dst = tiles[("res",) + group][:].rearrange("p (w u e) -> p w u e", u=2, e=2)
+                    src = tiles[group][:].rearrange("p (u w e) -> p w u e", u=2, e=2)
+                if engine == "vector":
+                    nc.vector.tensor_copy(out=dst, in_=src)
+                else:
+                    nc.scalar.copy(out=dst, in_=src)
+
+            step(engine, ("emptied",) + group, needs, emit)
+
+        def store0(b, j):
+            dst = out_0[b].rearrange("(p j) c -> p j c", j=PACK)[:, j, :]
+            step("sync", ("stored", "out0", b, j), [("emptied", "out0", b, j, ch) for ch in range(2)],
+                 lambda: nc.sync.dma_start(out=dst, in_=tiles["res0", b, j][:]))
+
+        def store1(r, h):
+            dst = out_1[r * P:(r + 1) * P, h * HALF:(h + 1) * HALF]
+            step("sync", ("stored", "out1", r, h), [("emptied", "out1", r, h)],
+                 lambda: nc.sync.dma_start(out=dst, in_=tiles["res", "out1", r, h][:]))
+
+        warm_in = sbuf("grp_scalar0", PACK * HALF, BF16)
+        warm = [sbuf("warm_c4", HALF, U32), sbuf("warm_s4", HALF, U8), sbuf("warm_c5", P, U32), sbuf("warm_s5", P, U8)]
+
+        def make_warm():
+            nc.vector.memset(warm_in[:], 1.0)
+            nc.vector.quantize_mx(out=warm[2][:].bitcast(E5), scales=warm[3][:], in_=warm_in[:, :HALF])
+            nc.vector.quantize_mx(out=warm[0][:].bitcast(E4), scales=warm[1][:], in_=warm_in[:])
+
+        def warm_up(n):
+            def emit():
+                for i in range(WARM[n]):
+                    acc = psum.tile([P, HALF], F32, name="bank%d" % (i % 2))
+                    nc.tensor.matmul_mx(out=acc[:], lhsT=warm[2][:].bitcast(E5), lhsT_scale=warm[3][:],
+                                        rhs=warm[0][:].bitcast(E4), rhs_scale=warm[1][:], start=True, stop=True)
+
+            step("tensor", ("warm", n), [("warm_made",)], emit)
+
+        t_count = [0]
+
+        def turn(name, pair):
+            transpose(name, pair, 4 + t_count[0] % 4)
+            t_count[0] = t_count[0] + 1
+            copy_transposed(name, pair)
+
+        def product0(b, j, ch, bank):
+            multiply(("out0", b, j, ch), [0, 1], bank)
+
+        warm_up(0)
+        turn(("dvt", 0, 0), 0)
+        turn(("dvt", 0, 0), 1)
+        turn(("dvt", 0, 1), 0)
+        turn(("dvt", 0, 1), 1)
+        turn(("w", 0, 0), 0)
+        turn(("w", 0, 1), 0)
+        turn(("w", 0, 0), 1)
+        turn(("w", 0, 1), 1)
+        turn(("w", 1, 0), 0)
+        turn(("w", 1, 1), 0)
+        warm_up(1)
+        turn(("w", 1, 0), 1)
+        turn(("w", 1, 1), 1)
+        turn(("dvt", 1, 0), 0)
+        turn(("dvt", 1, 0), 1)
+        product0(0, 0, 0, 0)
+        product0(0, 1, 0, 1)
+        turn(("dvt", 1, 1), 0)
+        turn(("dvt", 1, 1), 1)
+        product0(0, 2, 0, 2)
+        product0(0, 3, 0, 3)
+        for j in range(4):
+            empty(("out0", 0, j, 0))
+        for j in range(4):
+            product0(0, j, 1, j + 4)
+            empty(("out0", 0, j, 1))
+        for j in range(4):
+            for ch in range(2):
+                product0(1, j, ch, 2 * j + ch)
+                empty(("out0", 1, j, ch))
+        order1 = []
+        for r in range(4):
+            multiply(("out1", r, 0), [0, 1], r)
+        for r in range(4):
+            multiply(("out1", r, 1), [0], r + 4)
+        for r in range(4):
+            multiply(("out1", r, 1), [1])
+        for r in range(4):
+            multiply(("out1", r, 0), [2, 3])
+            order1.append((r, 0))
+        for r in range(4, 6):
+            multiply(("out1", r, 0), [0, 1], r - 4)
+        for r in range(4, 6):
+            multiply(("out1", r, 1), [0, 1], r - 2)
+        for r in range(4):
+            multiply(("out1", r, 1), [2])
+        for r in range(4, 6):
+            multiply(("out1", r, 0), [2, 3])
+            multiply(("out1", r, 1), [2])
+            order1.append((r, 0))
+        for r in range(6):
+            multiply(("out1", r, 1), [3])
+            order1.append((r, 1))
+        for r in range(6, 8):
+            multiply(("out1", r, 0), [0, 1], r - 6)
+        for r in range(6, 8):
+            multiply(("out1", r, 1), [0, 1], r - 2)
+        for h in range(2):
+            for r in range(6, 8):
+                multiply(("out1", r, h), [2, 3])
+                order1.append((r, h))
+        for i, cell in enumerate(order1):
+            for name, pos in zip(SCALAR_X, SPOS):
+                if pos == i:
+                    interleave("scalar", ("x",) + name)
+            if i not in VE:
+                empty(("out1",) + cell)
+        def il(name):
+            if (name[0] == "x" and name[1:] in SCALAR_X):
+                return
+            interleave("vector", name)
+
+        step("vector", ("warm_made",), [], make_warm)
+        step("vector", ("gates",), [], make_gates)
+        gate(0, 0, 0)
+        gate(1, 0, 0)
+        gate(0, 0, 1)
+        il(("dz", 0, 0))
+        quantise(("dvt", 0, 0))
+        gate(1, 0, 1, (0,))
+        quantise(("dvt", 0, 1))
+        il(("dz", 2, 0))
+        quantise(("w", 0, 0))
+        quantise(("w", 0, 1))
+        gate(0, 1, 0)
+        quantise(("dz", 0, 0))
+        gate(0, 1, 1)
+        quantise(("w", 1, 0))
+        quantise(("w", 1, 1))
+        quantise(("dvt", 1, 0))
+        il(("dz", 1, 0))
+        quantise(("dz", 2, 0))
+        quantise(("dz", 1, 0))
+        il(("x", 0, 0))
+        quantise(("dvt", 1, 1))
+        il(("x", 0, 1))
+        quantise(("x", 0, 0))
+        il(("dz", 0, 1))
+        quantise(("x", 0, 1))
+        il(("dz", 1, 1))
+        quantise(("dz", 0, 1))
+        gate(1, 1, 0, (0,))
+        gate(1, 1, 1, (0,))
+        quantise(("dz", 1, 1))
+        il(("dz", 3, 0))
+        gate(1, 0, 1, (1,))
+        quantise(("dz", 3, 0))
+        quantise(("x", 1, 0))
+        il(("x", 0, 2))
+        quantise(("x", 1, 1))
+        il(("dz", 2, 1))
+        quantise(("x", 0, 2))
+        gate(1, 1, 0, (1,))
+        gate(1, 1, 1, (1,))
+        quantise(("dz", 2, 1))
+        il(("dz", 3, 1))
+        quantise(("x", 1, 2))
+        il(("x", 0, 3))
+        quantise(("dz", 3, 1))
+        il(("x", 1, 3))
+        quantise(("x", 0, 3))
+        quantise(("x", 1, 3))
+        for i in VE:
+            empty(("out1",) + order1[i], "vector")
+        for b in range(B):
+            for j in range(4):
+                store0(b, j)
+        for cell in order1:
+            store1(*cell)
+
+        done = set()
+        heads = {engine: 0 for engine in queues}
+        left = sum(len(v) for v in queues.values())
+        while left:
+            before = left
+            for engine, steps in queues.items():
+                while heads[engine] < len(steps) and all(need in done for need in steps[heads[engine]][1]):
+                    key, needs, emit = steps[heads[engine]]
+                    emit()
+                    done.add(key)
+                    heads[engine] = heads[engine] + 1
+                    left = left - 1
+            assert left < before

@@ -19,10 +19,11 @@ P = 128
 PACK = 4
 HALF = 512
 ROWS = C // P
-SCALAR_X = ((1, 0), (1, 1), (1, 2))
+G_LOADS = ((0, 0, 1), (0, 1, 2), (0, 2, 4), (1, 0, 2), (1, 2, 4))
+SCALAR_X = ((1, 1), (0, 2), (0, 3))
 SPOS = (0, 0, 4)
-VE = (9, 11, 13, 15)
-WARM = (3, 0)
+VE = (11, 13, 15)
+WARM = (5, 2, 2, 2, 2)
 
 
 def tile_crossattention_for_fusion_temporal_pa_v_kernel(
@@ -56,9 +57,10 @@ def tile_crossattention_for_fusion_temporal_pa_v_kernel(
         eq = keep.tile([P, B, PACK], F32, name="eq")
         gates = [keep.tile([P, B, PACK], F32, name="gate%d" % s) for s in range(2)]
         w_raw = {(ch, rp): keep.tile([P, 2, DV], BF16, name="w%d%d" % (ch, rp)) for ch in range(2) for rp in range(2)}
-        g_raw = {(b, jp): keep.tile([P, 2, DV], BF16, name="g%d%d" % (b, jp)) for b in range(B) for jp in range(2)}
+        g_raw = {(b, j0): keep.tile([P, j1 - j0, DV], BF16, name="g%d%d" % (b, j0)) for b, j0, j1 in G_LOADS}
+        g_home = {(b, j): (b, j0) for b, j0, j1 in G_LOADS for j in range(j0, j1)}
         x_raw = keep.tile([P, 4, PACK, C], BF16, name="x")
-        dz = {(t, h): sbuf("dz%d%d" % (t, h), PACK * HALF, BF16) for t in range(4) for h in range(2)}
+        dz = [sbuf("dz%d" % t, PACK * DV, BF16) for t in range(4)]
         codes = {}
         scales = {}
         names = ([("w", ch, h) for ch in range(2) for h in range(2)] + [("dvt", b, h) for b in range(B) for h in range(2)]
@@ -77,18 +79,19 @@ def tile_crossattention_for_fusion_temporal_pa_v_kernel(
         def load_w(ch, rp):
             load(("load_w", ch, rp), w_raw[ch, rp][:], w_view[ch][:, 2 * rp:2 * rp + 2, :])
 
-        def load_g(b, jp):
-            load(("load_g", b, jp), g_raw[b, jp][:],
-                 grad_out[b].rearrange("(p j) d -> p j d", j=PACK)[:, 2 * jp:2 * jp + 2, :])
+        def load_g(n):
+            b, j0, j1 = G_LOADS[n]
+            load(("load_g", b, j0), g_raw[b, j0][:], grad_out[b].rearrange("(p j) d -> p j d", j=PACK)[:, j0:j1, :])
 
-        load_g(0, 0)
-        load_g(0, 1)
+        load_g(0)
+        load_g(1)
+        load_g(2)
         load_w(0, 0)
         load_w(0, 1)
         load_w(1, 0)
         load_w(1, 1)
-        load_g(1, 0)
-        load_g(1, 1)
+        load_g(3)
+        load_g(4)
         for t, src in enumerate([xs[0], xs[1], xis[0], xis[1]]):
             load(("load_x", t), x_raw[:, t], src.rearrange("(p j) c -> p j c", j=PACK))
 
@@ -96,46 +99,48 @@ def tile_crossattention_for_fusion_temporal_pa_v_kernel(
             nc.vector.tensor_tensor(out=gates[0][:], in0=rgb[:], in1=eq[:], op=ALU.add)
             nc.vector.tensor_scalar(out=gates[1][:], in0=rgb[:], scalar1=-1.0, scalar2=1.0, op0=ALU.mult, op1=ALU.add)
 
-        def gate(stream, b, jp, halves=(0, 1)):
-            for h in halves:
-                def emit(h=h):
-                    for i in range(2):
-                        j = 2 * jp + i
-                        nc.vector.tensor_scalar(
-                            out=dz[2 * stream + b, h][:, j * HALF:(j + 1) * HALF].rearrange("p (u w e) -> p u w e", u=2, e=2),
-                            in0=g_raw[b, jp][:, i, h * HALF:(h + 1) * HALF].rearrange("p (w u e) -> p u w e", u=2, e=2),
-                            scalar1=gates[stream][:, b, j:j + 1], scalar2=None, op0=ALU.mult)
+        def gate(stream, b, j):
+            home = g_home[b, j]
 
-                step("vector", ("gated", 2 * stream + b, h, jp), [("load_g", b, jp)], emit)
+            def emit():
+                nc.vector.tensor_scalar(
+                    out=dz[2 * stream + b][:, j * DV:(j + 1) * DV].rearrange("p (u w e) -> p u w e", u=2, e=2),
+                    in0=g_raw[home][:, j - home[1], :].rearrange("p (w u e) -> p u w e", u=2, e=2),
+                    scalar1=gates[stream][:, b, j:j + 1], scalar2=None, op0=ALU.mult)
+
+            step("vector", ("gated", 2 * stream + b, j), [("load_g",) + home], emit)
 
         counts = {"vector": 0, "scalar": 0, "t": 0, "r1": 0}
 
-        def interleave(engine, name):
-            slot = "grp_%s%d" % (engine, counts[engine] % 3)
-            counts[engine] = counts[engine] + 1
-            needs = reuse(slot, ("quantised",) + name)
+        def interleave(engine, name, part=0, parts=1):
+            needs = []
+            if part == 0:
+                slot = "grp_%s%d" % (engine, counts[engine] % 3)
+                counts[engine] = counts[engine] + 1
+                needs = reuse(slot, ("quantised",) + name)
             if name[0] == "dz":
                 t, h = name[1:]
-                needs = needs + [("gated", t, h, jp) for jp in range(2)]
+                needs = needs + [("gated", t, j) for j in range(PACK)]
             else:
                 needs = needs + [("load_x", 2 * name[1] + b) for b in range(B)]
 
             def emit():
-                grouped = sbuf(slot, PACK * HALF, BF16)
-                tiles[("grouped",) + name] = grouped
+                if part == 0:
+                    tiles[("grouped",) + name] = sbuf(slot, PACK * HALF, BF16)
+                grouped = tiles[("grouped",) + name]
                 if name[0] == "dz":
-                    src = dz[t, h][:].rearrange("p (j c i) -> p c j i", j=PACK, i=4)
-                    dst = grouped[:].rearrange("p (c i j) -> p c j i", j=PACK, i=4)
+                    src = dz[t][:].rearrange("p (j u h c i) -> p h u c j i", j=PACK, u=2, h=2, i=4)[:, h]
                 else:
                     s, rp = name[1:]
                     src = x_raw[:, 2 * s:2 * s + 2, :, rp * 2 * P:(rp + 1) * 2 * P].rearrange("p b j (c i) -> p b c j i", i=4)
-                    dst = grouped[:].rearrange("p (b c i j) -> p b c j i", b=B, j=PACK, i=4)
+                dst = grouped[:].rearrange("p (u c i j) -> p u c j i", u=2, j=PACK, i=4)
+                share = slice(part * 64 // parts, (part + 1) * 64 // parts)
                 if engine == "vector":
-                    nc.vector.tensor_copy(out=dst, in_=src)
+                    nc.vector.tensor_copy(out=dst[:, :, share], in_=src[:, :, share])
                 else:
-                    nc.scalar.copy(out=dst, in_=src)
+                    nc.scalar.copy(out=dst[:, :, share], in_=src[:, :, share])
 
-            step(engine, ("grouped",) + name, needs, emit)
+            step(engine, ("grouped",) + name + ((part,) if part + 1 < parts else ()), needs, emit)
 
         def quantise(name):
             fmt = E5 if name[0] in ("dz", "dvt") else E4
@@ -158,7 +163,7 @@ def tile_crossattention_for_fusion_temporal_pa_v_kernel(
                 needs = needs + [("load_w", ch, pair)]
             else:
                 b, jp = name[1:]
-                needs = needs + [("gated", b, pair, jp)]
+                needs = needs + [("gated", b, 2 * jp + i) for i in range(2)]
 
             def emit():
                 acc = psum.tile([P, 2, 2, P], F32, name="bank%d" % bank)
@@ -169,8 +174,8 @@ def tile_crossattention_for_fusion_temporal_pa_v_kernel(
                             row = w_raw[ch, pair][:, i, h * HALF:(h + 1) * HALF]
                             words = row.bitcast(F32)[:, u::2]
                         else:
-                            first = (2 * (2 * jp + i) + u) * P
-                            words = dz[b, pair][:].bitcast(F32)[:, first:first + P]
+                            first = (4 * (2 * jp + i) + 2 * u + pair) * P
+                            words = dz[b][:].bitcast(F32)[:, first:first + P]
                         nc.tensor.transpose(acc[:, i, u, :], words, ident[:])
 
             step("tensor", key, needs, emit)
@@ -257,13 +262,15 @@ def tile_crossattention_for_fusion_temporal_pa_v_kernel(
             step("sync", ("stored", "out1", r, h), [("emptied", "out1", r, h)],
                  lambda: nc.sync.dma_start(out=dst, in_=tiles["res", "out1", r, h][:]))
 
-        warm_in = sbuf("grp_scalar0", PACK * HALF, BF16)
+        warm_in = sbuf("warm_in", HALF, BF16)
         warm = [sbuf("warm_c4", HALF, U32), sbuf("warm_s4", HALF, U8), sbuf("warm_c5", P, U32), sbuf("warm_s5", P, U8)]
 
         def make_warm():
-            nc.vector.memset(warm_in[:], 1.0)
-            nc.vector.quantize_mx(out=warm[2][:].bitcast(E5), scales=warm[3][:], in_=warm_in[:, :HALF])
-            nc.vector.quantize_mx(out=warm[0][:].bitcast(E4), scales=warm[1][:], in_=warm_in[:])
+            nc.vector.memset(warm_in[:].bitcast(F32), 1.0)
+            nc.vector.quantize_mx(out=warm[2][:].bitcast(E5), scales=warm[3][:], in_=warm_in[:])
+            for i in range(4):
+                cols = slice(i * P, (i + 1) * P)
+                nc.vector.quantize_mx(out=warm[0][:, cols].bitcast(E4), scales=warm[1][:, cols], in_=warm_in[:])
 
         def warm_up(n):
             def emit():
@@ -287,61 +294,71 @@ def tile_crossattention_for_fusion_temporal_pa_v_kernel(
         warm_up(0)
         turn(("dvt", 0, 0), 0)
         turn(("dvt", 0, 0), 1)
+        warm_up(1)
         turn(("dvt", 0, 1), 0)
         turn(("dvt", 0, 1), 1)
+        interleave("scalar", ("dz", 2, 0), 0, 4)
+        warm_up(2)
         turn(("w", 0, 0), 0)
         turn(("w", 0, 1), 0)
+        interleave("scalar", ("dz", 2, 0), 1, 4)
+        warm_up(3)
         turn(("w", 0, 0), 1)
         turn(("w", 0, 1), 1)
+        interleave("scalar", ("dz", 2, 0), 2, 4)
+        warm_up(4)
         turn(("w", 1, 0), 0)
         turn(("w", 1, 1), 0)
-        warm_up(1)
+        interleave("scalar", ("dz", 2, 0), 3, 4)
+        product0(0, 0, 0, 0)
         turn(("w", 1, 0), 1)
         turn(("w", 1, 1), 1)
+        product0(0, 1, 0, 1)
+        empty(("out0", 0, 0, 0))
         turn(("dvt", 1, 0), 0)
         turn(("dvt", 1, 0), 1)
-        product0(0, 0, 0, 0)
-        product0(0, 1, 0, 1)
+        product0(0, 2, 0, 2)
+        empty(("out0", 0, 1, 0))
         turn(("dvt", 1, 1), 0)
         turn(("dvt", 1, 1), 1)
-        product0(0, 2, 0, 2)
         product0(0, 3, 0, 3)
-        for j in range(4):
+        for j in range(2, 4):
             empty(("out0", 0, j, 0))
         for j in range(4):
-            product0(0, j, 1, j + 4)
+            product0(0, j, 1, (0, 1, 4, 5)[j])
             empty(("out0", 0, j, 1))
         for j in range(4):
             for ch in range(2):
-                product0(1, j, ch, 2 * j + ch)
+                product0(1, j, ch, (6, 7, 2, 3, 0, 1, 4, 5)[2 * j + ch])
                 empty(("out0", 1, j, ch))
         order1 = []
         for r in range(4):
-            multiply(("out1", r, 0), [0, 1], r)
+            multiply(("out1", r, 0), [0, 1], (6, 7, 2, 3)[r])
         for r in range(4):
-            multiply(("out1", r, 1), [0], r + 4)
+            multiply(("out1", r, 1), [0], (0, 1, 4, 5)[r])
         for r in range(4):
             multiply(("out1", r, 1), [1])
         for r in range(4):
             multiply(("out1", r, 0), [2, 3])
             order1.append((r, 0))
         for r in range(4, 6):
-            multiply(("out1", r, 0), [0, 1], r - 4)
-        for r in range(4, 6):
-            multiply(("out1", r, 1), [0, 1], r - 2)
+            multiply(("out1", r, 0), [0, 1], r + 2)
         for r in range(4):
             multiply(("out1", r, 1), [2])
         for r in range(4, 6):
+            multiply(("out1", r, 1), [0, 1], r - 2)
+        for r in range(4, 6):
             multiply(("out1", r, 0), [2, 3])
-            multiply(("out1", r, 1), [2])
             order1.append((r, 0))
+        for r in range(4, 6):
+            multiply(("out1", r, 1), [2])
         for r in range(6):
             multiply(("out1", r, 1), [3])
             order1.append((r, 1))
         for r in range(6, 8):
-            multiply(("out1", r, 0), [0, 1], r - 6)
+            multiply(("out1", r, 0), [0, 1], r)
         for r in range(6, 8):
-            multiply(("out1", r, 1), [0, 1], r - 2)
+            multiply(("out1", r, 1), [0, 1], r - 6)
         for h in range(2):
             for r in range(6, 8):
                 multiply(("out1", r, h), [2, 3])
@@ -362,50 +379,50 @@ def tile_crossattention_for_fusion_temporal_pa_v_kernel(
         gate(0, 0, 0)
         gate(1, 0, 0)
         gate(0, 0, 1)
+        gate(1, 0, 1)
+        gate(0, 0, 2)
+        gate(0, 0, 3)
+        gate(1, 0, 2)
+        gate(1, 0, 3)
         il(("dz", 0, 0))
         quantise(("dvt", 0, 0))
-        gate(1, 0, 1, (0,))
+        il(("dz", 0, 1))
         quantise(("dvt", 0, 1))
-        il(("dz", 2, 0))
+        quantise(("dz", 0, 0))
         quantise(("w", 0, 0))
         quantise(("w", 0, 1))
-        gate(0, 1, 0)
-        quantise(("dz", 0, 0))
-        gate(0, 1, 1)
+        for j in range(4):
+            gate(0, 1, j)
+        quantise(("dz", 0, 1))
+        il(("dz", 1, 0))
         quantise(("w", 1, 0))
         quantise(("w", 1, 1))
-        quantise(("dvt", 1, 0))
-        il(("dz", 1, 0))
         quantise(("dz", 2, 0))
         quantise(("dz", 1, 0))
+        quantise(("dvt", 1, 0))
         il(("x", 0, 0))
         quantise(("dvt", 1, 1))
         il(("x", 0, 1))
         quantise(("x", 0, 0))
-        il(("dz", 0, 1))
-        quantise(("x", 0, 1))
         il(("dz", 1, 1))
-        quantise(("dz", 0, 1))
-        gate(1, 1, 0, (0,))
-        gate(1, 1, 1, (0,))
+        quantise(("x", 0, 1))
+        for j in range(4):
+            gate(1, 1, j)
         quantise(("dz", 1, 1))
         il(("dz", 3, 0))
-        gate(1, 0, 1, (1,))
+        il(("x", 1, 0))
         quantise(("dz", 3, 0))
         quantise(("x", 1, 0))
-        il(("x", 0, 2))
         quantise(("x", 1, 1))
         il(("dz", 2, 1))
         quantise(("x", 0, 2))
-        gate(1, 1, 0, (1,))
-        gate(1, 1, 1, (1,))
         quantise(("dz", 2, 1))
-        il(("dz", 3, 1))
+        il(("x", 1, 2))
         quantise(("x", 1, 2))
-        il(("x", 0, 3))
+        il(("dz", 3, 1))
+        quantise(("x", 0, 3))
         quantise(("dz", 3, 1))
         il(("x", 1, 3))
-        quantise(("x", 0, 3))
         quantise(("x", 1, 3))
         for i in VE:
             empty(("out1",) + order1[i], "vector")

@@ -4,7 +4,7 @@ import concourse.mybir as mybir
 from concourse.masks import make_identity
 
 B, N, C, DV = 2, 512, 1024, 1024
-FLOPS = 2 * B * N * C * DV * 3
+FLOPS = 3 * 2 * B * N * C * DV
 BYTES = 2 * (3 * B * N * C + C * DV) + 8 * B * N + 4 * (B * N * C + C * DV)
 
 F32 = mybir.dt.float32
@@ -18,12 +18,13 @@ ALU = mybir.AluOpType
 P = 128
 PACK = 4
 HALF = 512
-ROWS = C // P
+PASSES = 2 * B
 G_LOADS = ((0, 0, 1), (0, 1, 2), (0, 2, 4), (1, 0, 2), (1, 2, 4))
-SCALAR_X = ((1, 1), (0, 2), (0, 3))
-SPOS = (0, 0, 4)
-VE = (11, 13, 15)
-WARM = (5, 2, 2, 2, 2)
+WARM_FIRST, WARM_SECOND, WARM_LATER = 5, 1, 2
+INTERLEAVE_BUFS = 3
+TRANSPOSED_BUFS = 4
+RESULT_BUFS = 8
+QUARTERS = 4
 
 
 def tile_crossattention_for_fusion_temporal_pa_v_kernel(
@@ -40,15 +41,26 @@ def tile_crossattention_for_fusion_temporal_pa_v_kernel(
 
         queues = {"sync": [], "vector": [], "scalar": [], "tensor": []}
         tiles = {}
-        slot_free = {}
+        last_use = {}
+        taken = {"vector": 0, "scalar": 0, "transposed": 0, "result": 0}
 
         def step(engine, key, needs, emit):
-            queues[engine].append((key, list(needs), emit))
+            queues[engine].append((key, needs, emit))
 
-        def reuse(slot, release_key):
-            before = slot_free.get(slot)
-            slot_free[slot] = release_key
+        def reuse(buffer, freed_by):
+            before = last_use.get(buffer)
+            last_use[buffer] = freed_by
             return [] if before is None else [before]
+
+        def rotate(kind, count):
+            taken[kind] = taken[kind] + 1
+            return "%s%d" % (kind, (taken[kind] - 1) % count)
+
+        def copy(engine, dst, src):
+            if engine == "vector":
+                nc.vector.tensor_copy(out=dst, in_=src)
+            else:
+                nc.scalar.copy(out=dst, in_=src)
 
         ident = sbuf("ident", P, F32)
         make_identity(nc, ident[:])
@@ -59,39 +71,37 @@ def tile_crossattention_for_fusion_temporal_pa_v_kernel(
         w_raw = {(ch, rp): keep.tile([P, 2, DV], BF16, name="w%d%d" % (ch, rp)) for ch in range(2) for rp in range(2)}
         g_raw = {(b, j0): keep.tile([P, j1 - j0, DV], BF16, name="g%d%d" % (b, j0)) for b, j0, j1 in G_LOADS}
         g_home = {(b, j): (b, j0) for b, j0, j1 in G_LOADS for j in range(j0, j1)}
-        x_raw = keep.tile([P, 4, PACK, C], BF16, name="x")
-        dz = [sbuf("dz%d" % t, PACK * DV, BF16) for t in range(4)]
+        x_raw = keep.tile([P, PASSES, PACK, C], BF16, name="x")
+        dz = [sbuf("dz%d" % t, PACK * DV, BF16) for t in range(PASSES)]
+
+        operands = ([("w", ch, h) for ch in range(2) for h in range(2)]
+                    + [("dvt", b, jp) for b in range(B) for jp in range(2)]
+                    + [("dz", t, h) for t in range(PASSES) for h in range(2)]
+                    + [("x", s, rp) for s in range(2) for rp in range(4)])
         codes = {}
         scales = {}
-        names = ([("w", ch, h) for ch in range(2) for h in range(2)] + [("dvt", b, h) for b in range(B) for h in range(2)]
-                 + [("dz", t, h) for t in range(4) for h in range(2)] + [("x", s, rp) for s in range(2) for rp in range(4)])
-        for name in names:
-            label = "_".join(str(part) for part in name)
-            codes[name] = sbuf("c_" + label, HALF, U32)
-            scales[name] = sbuf("s_" + label, HALF, U8)
+        for operand in operands:
+            label = "_".join(str(part) for part in operand)
+            codes[operand] = sbuf("codes_" + label, HALF, U32)
+            scales[operand] = sbuf("scales_" + label, HALF, U8)
 
         def load(key, dst, src):
             step("sync", key, [], lambda: nc.sync.dma_start(out=dst, in_=src))
 
+        def load_g(b):
+            for load_b, j0, j1 in G_LOADS:
+                if load_b == b:
+                    rows = grad_out[b].rearrange("(p j) d -> p j d", j=PACK)
+                    load(("load_g", b, j0), g_raw[b, j0][:], rows[:, j0:j1, :])
+
         nc.scalar.dma_start(out=rgb[:], in_=rgb_ratio.rearrange("b (p j) -> p b j", j=PACK))
         nc.scalar.dma_start(out=eq[:], in_=eq_ratio.rearrange("b (p j) -> p b j", j=PACK))
-        w_view = Wv.rearrange("(ch r p) d -> ch p r d", ch=2, p=P)
-        def load_w(ch, rp):
-            load(("load_w", ch, rp), w_raw[ch, rp][:], w_view[ch][:, 2 * rp:2 * rp + 2, :])
-
-        def load_g(n):
-            b, j0, j1 = G_LOADS[n]
-            load(("load_g", b, j0), g_raw[b, j0][:], grad_out[b].rearrange("(p j) d -> p j d", j=PACK)[:, j0:j1, :])
-
         load_g(0)
+        w_view = Wv.rearrange("(ch r p) d -> ch p r d", ch=2, p=P)
+        for ch in range(2):
+            for rp in range(2):
+                load(("load_w", ch, rp), w_raw[ch, rp][:], w_view[ch][:, 2 * rp:2 * rp + 2, :])
         load_g(1)
-        load_g(2)
-        load_w(0, 0)
-        load_w(0, 1)
-        load_w(1, 0)
-        load_w(1, 1)
-        load_g(3)
-        load_g(4)
         for t, src in enumerate([xs[0], xs[1], xis[0], xis[1]]):
             load(("load_x", t), x_raw[:, t], src.rearrange("(p j) c -> p j c", j=PACK))
 
@@ -110,111 +120,100 @@ def tile_crossattention_for_fusion_temporal_pa_v_kernel(
 
             step("vector", ("gated", 2 * stream + b, j), [("load_g",) + home], emit)
 
-        counts = {"vector": 0, "scalar": 0, "t": 0, "r1": 0}
-
-        def interleave(engine, name, part=0, parts=1):
+        def interleave(engine, operand, part=0, parts=1):
             needs = []
             if part == 0:
-                slot = "grp_%s%d" % (engine, counts[engine] % 3)
-                counts[engine] = counts[engine] + 1
-                needs = reuse(slot, ("quantised",) + name)
-            if name[0] == "dz":
-                t, h = name[1:]
+                buffer = rotate(engine, INTERLEAVE_BUFS)
+                needs = reuse(buffer, ("quantised",) + operand)
+            if operand[0] == "dz":
+                t, h = operand[1:]
                 needs = needs + [("gated", t, j) for j in range(PACK)]
+                src = dz[t][:].rearrange("p (j u h c) -> p h u c j", j=PACK, u=2, h=2)[:, h]
             else:
-                needs = needs + [("load_x", 2 * name[1] + b) for b in range(B)]
+                s, rp = operand[1:]
+                needs = needs + [("load_x", 2 * s + b) for b in range(B)]
+                src = x_raw[:, 2 * s:2 * s + 2, :, rp * 2 * P:(rp + 1) * 2 * P].rearrange("p b j c -> p b c j")
+            share = slice(part * 2 * P // parts, (part + 1) * 2 * P // parts)
 
             def emit():
                 if part == 0:
-                    tiles[("grouped",) + name] = sbuf(slot, PACK * HALF, BF16)
-                grouped = tiles[("grouped",) + name]
-                if name[0] == "dz":
-                    src = dz[t][:].rearrange("p (j u h c i) -> p h u c j i", j=PACK, u=2, h=2, i=4)[:, h]
-                else:
-                    s, rp = name[1:]
-                    src = x_raw[:, 2 * s:2 * s + 2, :, rp * 2 * P:(rp + 1) * 2 * P].rearrange("p b j (c i) -> p b c j i", i=4)
-                dst = grouped[:].rearrange("p (u c i j) -> p u c j i", u=2, j=PACK, i=4)
-                share = slice(part * 64 // parts, (part + 1) * 64 // parts)
-                if engine == "vector":
-                    nc.vector.tensor_copy(out=dst[:, :, share], in_=src[:, :, share])
-                else:
-                    nc.scalar.copy(out=dst[:, :, share], in_=src[:, :, share])
+                    tiles["input", operand] = sbuf(buffer, PACK * HALF, BF16)
+                dst = tiles["input", operand][:].rearrange("p (run c j) -> p run c j", run=2, j=PACK)
+                copy(engine, dst[:, :, share], src[:, :, share])
 
-            step(engine, ("grouped",) + name + ((part,) if part + 1 < parts else ()), needs, emit)
+            step(engine, ("interleaved", operand, parts - 1 - part), needs, emit)
 
-        def quantise(name):
-            fmt = E5 if name[0] in ("dz", "dvt") else E4
-            if name[0] in ("w", "dvt"):
-                needs = [("copied",) + name + (pair,) for pair in range(2)]
+        def quantise(operand):
+            if operand[0] in ("w", "dvt"):
+                needs = [("copied", operand, pair) for pair in range(2)]
             else:
-                needs = [("grouped",) + name]
+                needs = [("interleaved", operand, 0)]
+            fmt = E5 if operand[0] in ("dz", "dvt") else E4
+            step("vector", ("quantised",) + operand, needs, lambda: nc.vector.quantize_mx(
+                out=codes[operand][:].bitcast(fmt), scales=scales[operand][:], in_=tiles["input", operand][:]))
 
-            def emit():
-                nc.vector.quantize_mx(out=codes[name][:].bitcast(fmt), scales=scales[name][:],
-                                      in_=tiles[("grouped",) + name][:])
+        free_banks = [4, 5, 6, 7, 2, 3]
+        bank_of = {}
 
-            step("vector", ("quantised",) + name, needs, emit)
+        def take_bank(user, freed_by):
+            bank_of[user] = free_banks[0]
+            free_banks.remove(bank_of[user])
+            return reuse(bank_of[user], freed_by)
 
-        def transpose(name, pair, bank):
-            key = ("transposed",) + name + (pair,)
-            needs = reuse("bank%d" % bank, ("copied",) + name + (pair,))
-            if name[0] == "w":
-                ch, h = name[1:]
+        def turn(operand, pair):
+            user = (operand, pair)
+            needs = take_bank(user, ("copied", operand, pair))
+            if operand[0] == "w":
+                ch, h = operand[1:]
                 needs = needs + [("load_w", ch, pair)]
+                rows = [w_raw[ch, pair][:, i, h * HALF:(h + 1) * HALF].bitcast(F32) for i in range(2)]
+                words = [[rows[i][:, u::2] for u in range(2)] for i in range(2)]
             else:
-                b, jp = name[1:]
+                b, jp = operand[1:]
                 needs = needs + [("gated", b, 2 * jp + i) for i in range(2)]
+                runs = dz[b][:].bitcast(F32).rearrange("p (j u h w) -> p j u h w", j=PACK, u=2, h=2)
+                words = [[runs[:, 2 * jp + i, u, pair, :] for u in range(2)] for i in range(2)]
 
-            def emit():
-                acc = psum.tile([P, 2, 2, P], F32, name="bank%d" % bank)
-                tiles[key] = acc
+            def emit_transposes():
+                tiles[user] = psum.tile([P, 2, 2, P], F32, name="bank%d" % bank_of[user])
                 for i in range(2):
                     for u in range(2):
-                        if name[0] == "w":
-                            row = w_raw[ch, pair][:, i, h * HALF:(h + 1) * HALF]
-                            words = row.bitcast(F32)[:, u::2]
-                        else:
-                            first = (4 * (2 * jp + i) + 2 * u + pair) * P
-                            words = dz[b][:].bitcast(F32)[:, first:first + P]
-                        nc.tensor.transpose(acc[:, i, u, :], words, ident[:])
+                        nc.tensor.transpose(tiles[user][:, i, u, :], words[i][u], ident[:])
 
-            step("tensor", key, needs, emit)
+            step("tensor", ("transposed", operand, pair), needs, emit_transposes)
 
-        def copy_transposed(name, pair):
-            needs = [("transposed",) + name + (pair,)]
+            needs = [("transposed", operand, pair)]
             if pair == 0:
-                slot = "grp_t%d" % (counts["t"] % 4)
-                counts["t"] = counts["t"] + 1
-                needs = needs + reuse(slot, ("quantised",) + name)
+                buffer = rotate("transposed", TRANSPOSED_BUFS)
+                needs = needs + reuse(buffer, ("quantised",) + operand)
 
-            def emit():
+            def emit_copy():
                 if pair == 0:
-                    tiles[("grouped",) + name] = sbuf(slot, PACK * HALF, BF16)
-                words = tiles[("grouped",) + name][:].bitcast(F32)[:, pair * HALF:(pair + 1) * HALF]
-                nc.scalar.copy(out=words.rearrange("p (i n u) -> p i n u", i=2, u=2),
-                               in_=tiles[("transposed",) + name + (pair,)][:].rearrange("p i u n -> p i n u"))
+                    tiles["input", operand] = sbuf(buffer, PACK * HALF, BF16)
+                dst = tiles["input", operand][:].bitcast(F32)[:, pair * HALF:(pair + 1) * HALF]
+                nc.scalar.copy(out=dst.rearrange("p (i n u) -> p i n u", i=2, u=2),
+                               in_=tiles[user][:].rearrange("p i u n -> p i n u"))
 
-            step("scalar", ("copied",) + name + (pair,), needs, emit)
+            step("scalar", ("copied", operand, pair), needs, emit_copy)
+            free_banks.append(bank_of[user])
 
-        def multiply(group, passes, bank=None):
-            last = 1 if group[0] == "out0" else 3
-            needs = []
-            if passes[0] == 0:
-                needs = reuse("bank%d" % bank, ("emptied",) + group)
-            operands = []
+        def multiply(group, passes):
+            last = 1 if group[0] == "out0" else PASSES - 1
+            needs = take_bank(group, ("emptied",) + group) if passes[0] == 0 else []
+            pairs = []
             for t in passes:
                 if group[0] == "out0":
                     b, j, ch = group[1:]
-                    operands.append((("dvt", b, j // 2), 2 * t + j % 2, E5, ("w", ch, t), E4))
+                    pairs.append((("dvt", b, j // 2), 2 * t + j % 2, E5, ("w", ch, t), E4))
                 else:
                     r, h = group[1:]
-                    operands.append((("x", t // 2, r // 2), 2 * (t % 2) + r % 2, E4, ("dz", t, h), E5))
-            needs = needs + [("quantised",) + o[0] for o in operands] + [("quantised",) + o[3] for o in operands]
+                    pairs.append((("x", t // 2, r // 2), 2 * (t % 2) + r % 2, E4, ("dz", t, h), E5))
+            needs = needs + [("quantised",) + pair[n] for pair in pairs for n in (0, 3)]
 
             def emit():
                 if passes[0] == 0:
-                    tiles[group] = psum.tile([P, HALF], F32, name="bank%d" % bank)
-                for t, (fixed, block, fixed_fmt, moving, moving_fmt) in zip(passes, operands):
+                    tiles[group] = psum.tile([P, HALF], F32, name="bank%d" % bank_of[group])
+                for t, (fixed, block, fixed_fmt, moving, moving_fmt) in zip(passes, pairs):
                     cols = slice(block * P, (block + 1) * P)
                     nc.tensor.matmul_mx(
                         out=tiles[group][:],
@@ -222,219 +221,184 @@ def tile_crossattention_for_fusion_temporal_pa_v_kernel(
                         rhs=codes[moving][:].bitcast(moving_fmt), rhs_scale=scales[moving][:],
                         start=(t == 0), stop=(t == last))
 
-            step("tensor", ("summed",) + group + (passes[-1],), needs, emit)
+            step("tensor", ("summed", group, last - passes[-1]), needs, emit)
 
-        def empty(group, engine="scalar"):
-            last = 1 if group[0] == "out0" else 3
-            needs = [("summed",) + group + (last,)]
-            if group[0] == "out1":
-                slot = "res1_%d" % (counts["r1"] % 8)
-                counts["r1"] = counts["r1"] + 1
-                needs = needs + reuse(slot, ("stored",) + group)
-            elif group[1] == 1:
-                needs = needs + [("transposed", "w", group[2] // 2, h, group[2] % 2) for h in range(2)]
+        def empty_out0(b, j, ch):
+            group = ("out0", b, j, ch)
+            needs = [("summed", group, 0)]
+            buffer = "rows%d" % j if b == 0 else "w%d%d" % (j // 2, j % 2)
+            if b == 1:
+                needs = needs + [("transposed", ("w", j // 2, h), j % 2) for h in range(2)]
 
             def emit():
-                if group[0] == "out0":
-                    b, j, ch = group[1:]
-                    if ch == 0:
-                        tiles["res0", b, j] = keep.tile([P, C], F32, name="res0_%d" % j if b == 0 else "w%d%d" % (j // 2, j % 2))
-                    dst = tiles["res0", b, j][:, ch * HALF:(ch + 1) * HALF]
-                    src = tiles[group][:]
-                else:
-                    tiles[("res",) + group] = sbuf(slot, HALF, F32)
-                    dst = tiles[("res",) + group][:].rearrange("p (w u e) -> p w u e", u=2, e=2)
-                    src = tiles[group][:].rearrange("p (u w e) -> p w u e", u=2, e=2)
-                if engine == "vector":
-                    nc.vector.tensor_copy(out=dst, in_=src)
-                else:
-                    nc.scalar.copy(out=dst, in_=src)
+                if ch == 0:
+                    tiles["rows", b, j] = keep.tile([P, C], F32, name=buffer)
+                nc.scalar.copy(out=tiles["rows", b, j][:, ch * HALF:(ch + 1) * HALF], in_=tiles[group][:])
+
+            step("scalar", ("emptied",) + group, needs, emit)
+            free_banks.append(bank_of[group])
+            if ch == 1:
+                dst = out_0[b].rearrange("(p j) c -> p j c", j=PACK)[:, j, :]
+                step("sync", ("stored",) + group, [("emptied",) + group],
+                     lambda: nc.sync.dma_start(out=dst, in_=tiles["rows", b, j][:]))
+
+        def empty_out1(r, h, engine="scalar"):
+            group = ("out1", r, h)
+            buffer = rotate("result", RESULT_BUFS)
+            needs = [("summed", group, 0)] + reuse(buffer, ("stored",) + group)
+
+            def emit():
+                tiles["result", group] = sbuf(buffer, HALF, F32)
+                copy(engine, tiles["result", group][:].rearrange("p (w u e) -> p w u e", u=2, e=2),
+                     tiles[group][:].rearrange("p (u w e) -> p w u e", u=2, e=2))
 
             step(engine, ("emptied",) + group, needs, emit)
-
-        def store0(b, j):
-            dst = out_0[b].rearrange("(p j) c -> p j c", j=PACK)[:, j, :]
-            step("sync", ("stored", "out0", b, j), [("emptied", "out0", b, j, ch) for ch in range(2)],
-                 lambda: nc.sync.dma_start(out=dst, in_=tiles["res0", b, j][:]))
-
-        def store1(r, h):
+            free_banks.append(bank_of[group])
             dst = out_1[r * P:(r + 1) * P, h * HALF:(h + 1) * HALF]
-            step("sync", ("stored", "out1", r, h), [("emptied", "out1", r, h)],
-                 lambda: nc.sync.dma_start(out=dst, in_=tiles["res", "out1", r, h][:]))
+            step("sync", ("stored",) + group, [("emptied",) + group],
+                 lambda: nc.sync.dma_start(out=dst, in_=tiles["result", group][:]))
 
         warm_in = sbuf("warm_in", HALF, BF16)
-        warm = [sbuf("warm_c4", HALF, U32), sbuf("warm_s4", HALF, U8), sbuf("warm_c5", P, U32), sbuf("warm_s5", P, U8)]
+        warm_moving = (sbuf("warm_codes4", HALF, U32), sbuf("warm_scales4", HALF, U8))
+        warm_fixed = (sbuf("warm_codes5", P, U32), sbuf("warm_scales5", P, U8))
 
-        def make_warm():
+        def make_warm_operands():
             nc.vector.memset(warm_in[:].bitcast(F32), 1.0)
-            nc.vector.quantize_mx(out=warm[2][:].bitcast(E5), scales=warm[3][:], in_=warm_in[:])
-            for i in range(4):
+            nc.vector.quantize_mx(out=warm_fixed[0][:].bitcast(E5), scales=warm_fixed[1][:], in_=warm_in[:])
+            for i in range(HALF // P):
                 cols = slice(i * P, (i + 1) * P)
-                nc.vector.quantize_mx(out=warm[0][:, cols].bitcast(E4), scales=warm[1][:, cols], in_=warm_in[:])
+                nc.vector.quantize_mx(out=warm_moving[0][:, cols].bitcast(E4), scales=warm_moving[1][:, cols],
+                                      in_=warm_in[:])
 
-        def warm_up(n):
+        def warm_up(count):
             def emit():
-                for i in range(WARM[n]):
+                for i in range(count):
                     acc = psum.tile([P, HALF], F32, name="bank%d" % (i % 2))
-                    nc.tensor.matmul_mx(out=acc[:], lhsT=warm[2][:].bitcast(E5), lhsT_scale=warm[3][:],
-                                        rhs=warm[0][:].bitcast(E4), rhs_scale=warm[1][:], start=True, stop=True)
+                    nc.tensor.matmul_mx(out=acc[:], lhsT=warm_fixed[0][:].bitcast(E5), lhsT_scale=warm_fixed[1][:],
+                                        rhs=warm_moving[0][:].bitcast(E4), rhs_scale=warm_moving[1][:],
+                                        start=True, stop=True)
 
-            step("tensor", ("warm", n), [("warm_made",)], emit)
+            step("tensor", ("warm", len(queues["tensor"])), [("warm_operands",)], emit)
 
-        t_count = [0]
+        def spread(operand):
+            interleave("vector", operand)
 
-        def turn(name, pair):
-            transpose(name, pair, 4 + t_count[0] % 4)
-            t_count[0] = t_count[0] + 1
-            copy_transposed(name, pair)
-
-        def product0(b, j, ch, bank):
-            multiply(("out0", b, j, ch), [0, 1], bank)
-
-        warm_up(0)
-        turn(("dvt", 0, 0), 0)
-        turn(("dvt", 0, 0), 1)
-        warm_up(1)
-        turn(("dvt", 0, 1), 0)
-        turn(("dvt", 0, 1), 1)
-        interleave("scalar", ("dz", 2, 0), 0, 4)
-        warm_up(2)
-        turn(("w", 0, 0), 0)
-        turn(("w", 0, 1), 0)
-        interleave("scalar", ("dz", 2, 0), 1, 4)
-        warm_up(3)
-        turn(("w", 0, 0), 1)
-        turn(("w", 0, 1), 1)
-        interleave("scalar", ("dz", 2, 0), 2, 4)
-        warm_up(4)
-        turn(("w", 1, 0), 0)
-        turn(("w", 1, 1), 0)
-        interleave("scalar", ("dz", 2, 0), 3, 4)
-        product0(0, 0, 0, 0)
-        turn(("w", 1, 0), 1)
-        turn(("w", 1, 1), 1)
-        product0(0, 1, 0, 1)
-        empty(("out0", 0, 0, 0))
-        turn(("dvt", 1, 0), 0)
-        turn(("dvt", 1, 0), 1)
-        product0(0, 2, 0, 2)
-        empty(("out0", 0, 1, 0))
-        turn(("dvt", 1, 1), 0)
-        turn(("dvt", 1, 1), 1)
-        product0(0, 3, 0, 3)
-        for j in range(2, 4):
-            empty(("out0", 0, j, 0))
-        for j in range(4):
-            product0(0, j, 1, (0, 1, 4, 5)[j])
-            empty(("out0", 0, j, 1))
-        for j in range(4):
-            for ch in range(2):
-                product0(1, j, ch, (6, 7, 2, 3, 0, 1, 4, 5)[2 * j + ch])
-                empty(("out0", 1, j, ch))
-        order1 = []
-        for r in range(4):
-            multiply(("out1", r, 0), [0, 1], (6, 7, 2, 3)[r])
-        for r in range(4):
-            multiply(("out1", r, 1), [0], (0, 1, 4, 5)[r])
-        for r in range(4):
-            multiply(("out1", r, 1), [1])
-        for r in range(4):
-            multiply(("out1", r, 0), [2, 3])
-            order1.append((r, 0))
-        for r in range(4, 6):
-            multiply(("out1", r, 0), [0, 1], r + 2)
-        for r in range(4):
-            multiply(("out1", r, 1), [2])
-        for r in range(4, 6):
-            multiply(("out1", r, 1), [0, 1], r - 2)
-        for r in range(4, 6):
-            multiply(("out1", r, 0), [2, 3])
-            order1.append((r, 0))
-        for r in range(4, 6):
-            multiply(("out1", r, 1), [2])
-        for r in range(6):
-            multiply(("out1", r, 1), [3])
-            order1.append((r, 1))
-        for r in range(6, 8):
-            multiply(("out1", r, 0), [0, 1], r)
-        for r in range(6, 8):
-            multiply(("out1", r, 1), [0, 1], r - 6)
-        for h in range(2):
-            for r in range(6, 8):
-                multiply(("out1", r, h), [2, 3])
-                order1.append((r, h))
-        for i, cell in enumerate(order1):
-            for name, pos in zip(SCALAR_X, SPOS):
-                if pos == i:
-                    interleave("scalar", ("x",) + name)
-            if i not in VE:
-                empty(("out1",) + cell)
-        def il(name):
-            if (name[0] == "x" and name[1:] in SCALAR_X):
-                return
-            interleave("vector", name)
-
-        step("vector", ("warm_made",), [], make_warm)
+        step("vector", ("warm_operands",), [], make_warm_operands)
         step("vector", ("gates",), [], make_gates)
-        gate(0, 0, 0)
-        gate(1, 0, 0)
-        gate(0, 0, 1)
-        gate(1, 0, 1)
-        gate(0, 0, 2)
-        gate(0, 0, 3)
-        gate(1, 0, 2)
-        gate(1, 0, 3)
-        il(("dz", 0, 0))
+        for j in range(2):
+            gate(0, 0, j)
+            gate(1, 0, j)
+        for stream in range(2):
+            gate(stream, 0, 2)
+            gate(stream, 0, 3)
+        spread(("dz", 0, 0))
         quantise(("dvt", 0, 0))
-        il(("dz", 0, 1))
+        spread(("dz", 0, 1))
         quantise(("dvt", 0, 1))
         quantise(("dz", 0, 0))
         quantise(("w", 0, 0))
         quantise(("w", 0, 1))
-        for j in range(4):
+        for j in range(PACK):
             gate(0, 1, j)
         quantise(("dz", 0, 1))
-        il(("dz", 1, 0))
+        spread(("dz", 1, 0))
         quantise(("w", 1, 0))
         quantise(("w", 1, 1))
         quantise(("dz", 2, 0))
         quantise(("dz", 1, 0))
         quantise(("dvt", 1, 0))
-        il(("x", 0, 0))
+        spread(("x", 0, 0))
         quantise(("dvt", 1, 1))
-        il(("x", 0, 1))
+        spread(("x", 0, 1))
         quantise(("x", 0, 0))
-        il(("dz", 1, 1))
+        spread(("dz", 1, 1))
         quantise(("x", 0, 1))
-        for j in range(4):
+        for j in range(PACK):
             gate(1, 1, j)
         quantise(("dz", 1, 1))
-        il(("dz", 3, 0))
-        il(("x", 1, 0))
+        spread(("dz", 3, 0))
+        spread(("x", 1, 0))
         quantise(("dz", 3, 0))
         quantise(("x", 1, 0))
         quantise(("x", 1, 1))
-        il(("dz", 2, 1))
+        spread(("dz", 2, 1))
         quantise(("x", 0, 2))
         quantise(("dz", 2, 1))
-        il(("x", 1, 2))
+        spread(("x", 1, 2))
         quantise(("x", 1, 2))
-        il(("dz", 3, 1))
+        spread(("dz", 3, 1))
         quantise(("x", 0, 3))
         quantise(("dz", 3, 1))
-        il(("x", 1, 3))
+        spread(("x", 1, 3))
         quantise(("x", 1, 3))
-        for i in VE:
-            empty(("out1",) + order1[i], "vector")
-        for b in range(B):
-            for j in range(4):
-                store0(b, j)
-        for cell in order1:
-            store1(*cell)
+
+        warm_up(WARM_FIRST)
+        for pair in range(2):
+            turn(("dvt", 0, 0), pair)
+        warm_up(WARM_SECOND)
+        for pair in range(2):
+            turn(("dvt", 0, 1), pair)
+        for quarter, (ch, rp) in enumerate([(0, 0), (0, 1), (1, 0)]):
+            interleave("scalar", ("dz", 2, 0), quarter, QUARTERS)
+            warm_up(WARM_LATER)
+            for h in range(2):
+                turn(("w", ch, h), rp)
+        interleave("scalar", ("dz", 2, 0), QUARTERS - 1, QUARTERS)
+        free_banks.extend([0, 1])
+        multiply(("out0", 0, 0, 0), [0, 1])
+        for h in range(2):
+            turn(("w", 1, h), 1)
+        for jp in range(2):
+            multiply(("out0", 0, jp + 1, 0), [0, 1])
+            empty_out0(0, jp, 0)
+            for pair in range(2):
+                turn(("dvt", 1, jp), pair)
+        multiply(("out0", 0, 3, 0), [0, 1])
+        for j in (2, 3):
+            empty_out0(0, j, 0)
+        for b, j, ch in [(0, j, 1) for j in range(PACK)] + [(1, j, ch) for j in range(PACK) for ch in range(2)]:
+            multiply(("out0", b, j, ch), [0, 1])
+            empty_out0(b, j, ch)
+
+        for r in range(4):
+            multiply(("out1", r, 0), [0, 1])
+        for t in range(2):
+            for r in range(4):
+                multiply(("out1", r, 1), [t])
+        interleave("scalar", ("x", 1, 1))
+        interleave("scalar", ("x", 0, 2))
+        for r in range(4):
+            multiply(("out1", r, 0), [2, 3])
+            empty_out1(r, 0)
+        interleave("scalar", ("x", 0, 3))
+        for r in (4, 5):
+            multiply(("out1", r, 0), [0, 1])
+        for r in range(4):
+            multiply(("out1", r, 1), [2])
+        for r in (4, 5):
+            multiply(("out1", r, 1), [0, 1])
+        for r in (4, 5):
+            multiply(("out1", r, 0), [2, 3])
+            empty_out1(r, 0)
+        for r in (4, 5):
+            multiply(("out1", r, 1), [2])
+        for r in range(6):
+            multiply(("out1", r, 1), [3])
+            empty_out1(r, 1, "vector" if r == 5 else "scalar")
+        for r in (6, 7):
+            multiply(("out1", r, 0), [0, 1])
+        multiply(("out1", 6, 1), [0, 1])
+        for r in (6, 7):
+            multiply(("out1", r, 0), [2, 3])
+            empty_out1(r, 0, "vector" if r == 7 else "scalar")
+        multiply(("out1", 6, 1), [2, 3])
+        empty_out1(6, 1)
+        multiply(("out1", 7, 1), [0, 1, 2, 3])
+        empty_out1(7, 1, "vector")
 
         done = set()
         heads = {engine: 0 for engine in queues}
-        left = sum(len(v) for v in queues.values())
+        left = sum(len(steps) for steps in queues.values())
         while left:
             before = left
             for engine, steps in queues.items():

@@ -20,10 +20,12 @@ PACK = 4
 HALF = 512
 PASSES = 2 * B
 G_LOADS = ((0, 0, 1), (0, 1, 2), (0, 2, 4), (1, 0, 2), (1, 2, 4))
-WARM_FIRST, WARM_SECOND, WARM_LATER = 5, 1, 2
+WARM_FIRST = 6
+WARM_BETWEEN = 2
 INTERLEAVE_BUFS = 3
 TRANSPOSED_BUFS = 4
 RESULT_BUFS = 8
+NEIGHBOURS = 4
 QUARTERS = 4
 
 
@@ -128,17 +130,19 @@ def tile_crossattention_for_fusion_temporal_pa_v_kernel(
             if operand[0] == "dz":
                 t, h = operand[1:]
                 needs = needs + [("gated", t, j) for j in range(PACK)]
-                src = dz[t][:].rearrange("p (j u h c) -> p h u c j", j=PACK, u=2, h=2)[:, h]
+                src = dz[t][:].rearrange("p (j u h c i) -> p h u c j i", j=PACK, u=2, h=2, i=NEIGHBOURS)[:, h]
             else:
                 s, rp = operand[1:]
                 needs = needs + [("load_x", 2 * s + b) for b in range(B)]
-                src = x_raw[:, 2 * s:2 * s + 2, :, rp * 2 * P:(rp + 1) * 2 * P].rearrange("p b j c -> p b c j")
-            share = slice(part * 2 * P // parts, (part + 1) * 2 * P // parts)
+                src = x_raw[:, 2 * s:2 * s + 2, :, rp * 2 * P:(rp + 1) * 2 * P].rearrange(
+                    "p b j (c i) -> p b c j i", i=NEIGHBOURS)
+            groups = 2 * P // NEIGHBOURS
+            share = slice(part * groups // parts, (part + 1) * groups // parts)
 
             def emit():
                 if part == 0:
                     tiles["input", operand] = sbuf(buffer, PACK * HALF, BF16)
-                dst = tiles["input", operand][:].rearrange("p (run c j) -> p run c j", run=2, j=PACK)
+                dst = tiles["input", operand][:].rearrange("p (run c i j) -> p run c j i", run=2, j=PACK, i=NEIGHBOURS)
                 copy(engine, dst[:, :, share], src[:, :, share])
 
             step(engine, ("interleaved", operand, parts - 1 - part), needs, emit)
@@ -291,19 +295,18 @@ def tile_crossattention_for_fusion_temporal_pa_v_kernel(
         for stream in range(2):
             gate(stream, 0, 2)
             gate(stream, 0, 3)
-        spread(("dz", 0, 0))
-        quantise(("dvt", 0, 0))
-        spread(("dz", 0, 1))
-        quantise(("dvt", 0, 1))
-        quantise(("dz", 0, 0))
-        quantise(("w", 0, 0))
-        quantise(("w", 0, 1))
+        for n in range(2):
+            spread(("dz", 0, n))
+            quantise(("dvt", 0, n))
+        for h in range(2):
+            quantise(("dz", 0, h))
+        for h in range(2):
+            quantise(("w", 0, h))
         for j in range(PACK):
             gate(0, 1, j)
-        quantise(("dz", 0, 1))
         spread(("dz", 1, 0))
-        quantise(("w", 1, 0))
-        quantise(("w", 1, 1))
+        for h in range(2):
+            quantise(("w", 1, h))
         quantise(("dz", 2, 0))
         quantise(("dz", 1, 0))
         quantise(("dvt", 1, 0))
@@ -321,11 +324,11 @@ def tile_crossattention_for_fusion_temporal_pa_v_kernel(
         quantise(("dz", 3, 0))
         quantise(("x", 1, 0))
         quantise(("x", 1, 1))
-        spread(("dz", 2, 1))
-        quantise(("x", 0, 2))
-        quantise(("dz", 2, 1))
         spread(("x", 1, 2))
+        quantise(("x", 0, 2))
         quantise(("x", 1, 2))
+        spread(("dz", 2, 1))
+        quantise(("dz", 2, 1))
         spread(("dz", 3, 1))
         quantise(("x", 0, 3))
         quantise(("dz", 3, 1))
@@ -335,12 +338,12 @@ def tile_crossattention_for_fusion_temporal_pa_v_kernel(
         warm_up(WARM_FIRST)
         for pair in range(2):
             turn(("dvt", 0, 0), pair)
-        warm_up(WARM_SECOND)
+        warm_up(WARM_BETWEEN)
         for pair in range(2):
             turn(("dvt", 0, 1), pair)
         for quarter, (ch, rp) in enumerate([(0, 0), (0, 1), (1, 0)]):
             interleave("scalar", ("dz", 2, 0), quarter, QUARTERS)
-            warm_up(WARM_LATER)
+            warm_up(WARM_BETWEEN)
             for h in range(2):
                 turn(("w", ch, h), rp)
         interleave("scalar", ("dz", 2, 0), QUARTERS - 1, QUARTERS)
@@ -373,14 +376,12 @@ def tile_crossattention_for_fusion_temporal_pa_v_kernel(
         interleave("scalar", ("x", 0, 3))
         for r in (4, 5):
             multiply(("out1", r, 0), [0, 1])
-        for r in range(4):
-            multiply(("out1", r, 1), [2])
-        for r in (4, 5):
-            multiply(("out1", r, 1), [0, 1])
         for r in (4, 5):
             multiply(("out1", r, 0), [2, 3])
             empty_out1(r, 0)
         for r in (4, 5):
+            multiply(("out1", r, 1), [0, 1])
+        for r in range(6):
             multiply(("out1", r, 1), [2])
         for r in range(6):
             multiply(("out1", r, 1), [3])

from contextlib import ExitStack

import concourse.mybir as mybir
from concourse.masks import make_identity

B, N, C, DV = 2, 512, 1024, 1024
FLOPS = 3 * 2 * B * N * C * DV
BYTES = 2 * (3 * B * N * C + C * DV) + 8 * B * N + 4 * (B * N * C + C * DV)

F32 = mybir.dt.float32
BF16 = mybir.dt.bfloat16
U32 = mybir.dt.uint32
U8 = mybir.dt.uint8
E4 = mybir.dt.float8_e4m3fn_x4
E5 = mybir.dt.float8_e5m2_x4
ALU = mybir.AluOpType

P = 128
PACK = 4
HALF = 512
PASSES = 2 * B
G_LOADS = ((0, 0, 1), (0, 1, 2), (0, 2, 4), (1, 0, 2), (1, 2, 4))
WARM_FIRST = 6
WARM_BETWEEN = 2
INTERLEAVE_BUFS = 3
TRANSPOSED_BUFS = 4
RESULT_BUFS = 8
NEIGHBOURS = 4
QUARTERS = 4


def tile_crossattention_for_fusion_temporal_pa_v_kernel(
    tc, q, k, ki, xs, xis, Wv, rgb_ratio, eq_ratio, grad_out, out_0, out_1
):
    nc = tc.nc
    with ExitStack() as ctx:
        keep = ctx.enter_context(tc.tile_pool(name="keep", bufs=1))
        psum = ctx.enter_context(tc.psum_pool(name="psum", bufs=1))
        ctx.enter_context(tc.manual_schedule())

        def sbuf(name, width, dtype):
            return keep.tile([P, width], dtype, name=name, align_bytes=64)

        queues = {"sync": [], "vector": [], "scalar": [], "tensor": []}
        tiles = {}
        last_use = {}
        taken = {"vector": 0, "scalar": 0, "transposed": 0, "result": 0}

        def step(engine, key, needs, emit):
            queues[engine].append((key, needs, emit))

        def reuse(buffer, freed_by):
            before = last_use.get(buffer)
            last_use[buffer] = freed_by
            return [] if before is None else [before]

        def rotate(kind, count):
            taken[kind] = taken[kind] + 1
            return "%s%d" % (kind, (taken[kind] - 1) % count)

        def copy(engine, dst, src):
            if engine == "vector":
                nc.vector.tensor_copy(out=dst, in_=src)
            else:
                nc.scalar.copy(out=dst, in_=src)

        ident = sbuf("ident", P, F32)
        make_identity(nc, ident[:])

        rgb = keep.tile([P, B, PACK], F32, name="rgb")
        eq = keep.tile([P, B, PACK], F32, name="eq")
        gates = [keep.tile([P, B, PACK], F32, name="gate%d" % s) for s in range(2)]
        w_raw = {(ch, rp): keep.tile([P, 2, DV], BF16, name="w%d%d" % (ch, rp)) for ch in range(2) for rp in range(2)}
        g_raw = {(b, j0): keep.tile([P, j1 - j0, DV], BF16, name="g%d%d" % (b, j0)) for b, j0, j1 in G_LOADS}
        g_home = {(b, j): (b, j0) for b, j0, j1 in G_LOADS for j in range(j0, j1)}
        x_raw = keep.tile([P, PASSES, PACK, C], BF16, name="x")
        dz = [sbuf("dz%d" % t, PACK * DV, BF16) for t in range(PASSES)]

        operands = ([("w", ch, h) for ch in range(2) for h in range(2)]
                    + [("dvt", b, jp) for b in range(B) for jp in range(2)]
                    + [("dz", t, h) for t in range(PASSES) for h in range(2)]
                    + [("x", s, rp) for s in range(2) for rp in range(4)])
        codes = {}
        scales = {}
        for operand in operands:
            label = "_".join(str(part) for part in operand)
            codes[operand] = sbuf("codes_" + label, HALF, U32)
            scales[operand] = sbuf("scales_" + label, HALF, U8)

        def load(key, dst, src):
            step("sync", key, [], lambda: nc.sync.dma_start(out=dst, in_=src))

        def load_g(b):
            for load_b, j0, j1 in G_LOADS:
                if load_b == b:
                    rows = grad_out[b].rearrange("(p j) d -> p j d", j=PACK)
                    load(("load_g", b, j0), g_raw[b, j0][:], rows[:, j0:j1, :])

        nc.scalar.dma_start(out=rgb[:], in_=rgb_ratio.rearrange("b (p j) -> p b j", j=PACK))
        nc.scalar.dma_start(out=eq[:], in_=eq_ratio.rearrange("b (p j) -> p b j", j=PACK))
        load_g(0)
        w_view = Wv.rearrange("(ch r p) d -> ch p r d", ch=2, p=P)
        for ch in range(2):
            for rp in range(2):
                load(("load_w", ch, rp), w_raw[ch, rp][:], w_view[ch][:, 2 * rp:2 * rp + 2, :])
        load_g(1)
        for t, src in enumerate([xs[0], xs[1], xis[0], xis[1]]):
            load(("load_x", t), x_raw[:, t], src.rearrange("(p j) c -> p j c", j=PACK))

        def make_gates():
            nc.vector.tensor_tensor(out=gates[0][:], in0=rgb[:], in1=eq[:], op=ALU.add)
            nc.vector.tensor_scalar(out=gates[1][:], in0=rgb[:], scalar1=-1.0, scalar2=1.0, op0=ALU.mult, op1=ALU.add)

        def gate(stream, b, j):
            home = g_home[b, j]

            def emit():
                nc.vector.tensor_scalar(
                    out=dz[2 * stream + b][:, j * DV:(j + 1) * DV].rearrange("p (u w e) -> p u w e", u=2, e=2),
                    in0=g_raw[home][:, j - home[1], :].rearrange("p (w u e) -> p u w e", u=2, e=2),
                    scalar1=gates[stream][:, b, j:j + 1], scalar2=None, op0=ALU.mult)

            step("vector", ("gated", 2 * stream + b, j), [("load_g",) + home], emit)

        def interleave(engine, operand, part=0, parts=1):
            needs = []
            if part == 0:
                buffer = rotate(engine, INTERLEAVE_BUFS)
                needs = reuse(buffer, ("quantised",) + operand)
            if operand[0] == "dz":
                t, h = operand[1:]
                needs = needs + [("gated", t, j) for j in range(PACK)]
                src = dz[t][:].rearrange("p (j u h c i) -> p h u c j i", j=PACK, u=2, h=2, i=NEIGHBOURS)[:, h]
            else:
                s, rp = operand[1:]
                needs = needs + [("load_x", 2 * s + b) for b in range(B)]
                src = x_raw[:, 2 * s:2 * s + 2, :, rp * 2 * P:(rp + 1) * 2 * P].rearrange(
                    "p b j (c i) -> p b c j i", i=NEIGHBOURS)
            groups = 2 * P // NEIGHBOURS
            share = slice(part * groups // parts, (part + 1) * groups // parts)

            def emit():
                if part == 0:
                    tiles["input", operand] = sbuf(buffer, PACK * HALF, BF16)
                dst = tiles["input", operand][:].rearrange("p (run c i j) -> p run c j i", run=2, j=PACK, i=NEIGHBOURS)
                copy(engine, dst[:, :, share], src[:, :, share])

            step(engine, ("interleaved", operand, parts - 1 - part), needs, emit)

        def quantise(operand):
            if operand[0] in ("w", "dvt"):
                needs = [("copied", operand, pair) for pair in range(2)]
            else:
                needs = [("interleaved", operand, 0)]
            fmt = E5 if operand[0] in ("dz", "dvt") else E4
            step("vector", ("quantised",) + operand, needs, lambda: nc.vector.quantize_mx(
                out=codes[operand][:].bitcast(fmt), scales=scales[operand][:], in_=tiles["input", operand][:]))

        free_banks = [4, 5, 6, 7, 2, 3]
        bank_of = {}

        def take_bank(user, freed_by):
            bank_of[user] = free_banks[0]
            free_banks.remove(bank_of[user])
            return reuse(bank_of[user], freed_by)

        def turn(operand, pair):
            user = (operand, pair)
            needs = take_bank(user, ("copied", operand, pair))
            if operand[0] == "w":
                ch, h = operand[1:]
                needs = needs + [("load_w", ch, pair)]
                rows = [w_raw[ch, pair][:, i, h * HALF:(h + 1) * HALF].bitcast(F32) for i in range(2)]
                words = [[rows[i][:, u::2] for u in range(2)] for i in range(2)]
            else:
                b, jp = operand[1:]
                needs = needs + [("gated", b, 2 * jp + i) for i in range(2)]
                runs = dz[b][:].bitcast(F32).rearrange("p (j u h w) -> p j u h w", j=PACK, u=2, h=2)
                words = [[runs[:, 2 * jp + i, u, pair, :] for u in range(2)] for i in range(2)]

            def emit_transposes():
                tiles[user] = psum.tile([P, 2, 2, P], F32, name="bank%d" % bank_of[user])
                for i in range(2):
                    for u in range(2):
                        nc.tensor.transpose(tiles[user][:, i, u, :], words[i][u], ident[:])

            step("tensor", ("transposed", operand, pair), needs, emit_transposes)

            needs = [("transposed", operand, pair)]
            if pair == 0:
                buffer = rotate("transposed", TRANSPOSED_BUFS)
                needs = needs + reuse(buffer, ("quantised",) + operand)

            def emit_copy():
                if pair == 0:
                    tiles["input", operand] = sbuf(buffer, PACK * HALF, BF16)
                dst = tiles["input", operand][:].bitcast(F32)[:, pair * HALF:(pair + 1) * HALF]
                nc.scalar.copy(out=dst.rearrange("p (i n u) -> p i n u", i=2, u=2),
                               in_=tiles[user][:].rearrange("p i u n -> p i n u"))

            step("scalar", ("copied", operand, pair), needs, emit_copy)
            free_banks.append(bank_of[user])

        def multiply(group, passes):
            last = 1 if group[0] == "out0" else PASSES - 1
            needs = take_bank(group, ("emptied",) + group) if passes[0] == 0 else []
            pairs = []
            for t in passes:
                if group[0] == "out0":
                    b, j, ch = group[1:]
                    pairs.append((("dvt", b, j // 2), 2 * t + j % 2, E5, ("w", ch, t), E4))
                else:
                    r, h = group[1:]
                    pairs.append((("x", t // 2, r // 2), 2 * (t % 2) + r % 2, E4, ("dz", t, h), E5))
            needs = needs + [("quantised",) + pair[n] for pair in pairs for n in (0, 3)]

            def emit():
                if passes[0] == 0:
                    tiles[group] = psum.tile([P, HALF], F32, name="bank%d" % bank_of[group])
                for t, (fixed, block, fixed_fmt, moving, moving_fmt) in zip(passes, pairs):
                    cols = slice(block * P, (block + 1) * P)
                    nc.tensor.matmul_mx(
                        out=tiles[group][:],
                        lhsT=codes[fixed][:, cols].bitcast(fixed_fmt), lhsT_scale=scales[fixed][:, cols],
                        rhs=codes[moving][:].bitcast(moving_fmt), rhs_scale=scales[moving][:],
                        start=(t == 0), stop=(t == last))

            step("tensor", ("summed", group, last - passes[-1]), needs, emit)

        def empty_out0(b, j, ch):
            group = ("out0", b, j, ch)
            needs = [("summed", group, 0)]
            buffer = "rows%d" % j if b == 0 else "w%d%d" % (j // 2, j % 2)
            if b == 1:
                needs = needs + [("transposed", ("w", j // 2, h), j % 2) for h in range(2)]

            def emit():
                if ch == 0:
                    tiles["rows", b, j] = keep.tile([P, C], F32, name=buffer)
                nc.scalar.copy(out=tiles["rows", b, j][:, ch * HALF:(ch + 1) * HALF], in_=tiles[group][:])

            step("scalar", ("emptied",) + group, needs, emit)
            free_banks.append(bank_of[group])
            if ch == 1:
                dst = out_0[b].rearrange("(p j) c -> p j c", j=PACK)[:, j, :]
                step("sync", ("stored",) + group, [("emptied",) + group],
                     lambda: nc.sync.dma_start(out=dst, in_=tiles["rows", b, j][:]))

        def empty_out1(r, h, engine="scalar"):
            group = ("out1", r, h)
            buffer = rotate("result", RESULT_BUFS)
            needs = [("summed", group, 0)] + reuse(buffer, ("stored",) + group)

            def emit():
                tiles["result", group] = sbuf(buffer, HALF, F32)
                copy(engine, tiles["result", group][:].rearrange("p (w u e) -> p w u e", u=2, e=2),
                     tiles[group][:].rearrange("p (u w e) -> p w u e", u=2, e=2))

            step(engine, ("emptied",) + group, needs, emit)
            free_banks.append(bank_of[group])
            dst = out_1[r * P:(r + 1) * P, h * HALF:(h + 1) * HALF]
            step("sync", ("stored",) + group, [("emptied",) + group],
                 lambda: nc.sync.dma_start(out=dst, in_=tiles["result", group][:]))

        warm_in = sbuf("warm_in", HALF, BF16)
        warm_moving = (sbuf("warm_codes4", HALF, U32), sbuf("warm_scales4", HALF, U8))
        warm_fixed = (sbuf("warm_codes5", P, U32), sbuf("warm_scales5", P, U8))

        def make_warm_operands():
            nc.vector.memset(warm_in[:].bitcast(F32), 1.0)
            nc.vector.quantize_mx(out=warm_fixed[0][:].bitcast(E5), scales=warm_fixed[1][:], in_=warm_in[:])
            for i in range(HALF // P):
                cols = slice(i * P, (i + 1) * P)
                nc.vector.quantize_mx(out=warm_moving[0][:, cols].bitcast(E4), scales=warm_moving[1][:, cols],
                                      in_=warm_in[:])

        def warm_up(count):
            def emit():
                for i in range(count):
                    acc = psum.tile([P, HALF], F32, name="bank%d" % (i % 2))
                    nc.tensor.matmul_mx(out=acc[:], lhsT=warm_fixed[0][:].bitcast(E5), lhsT_scale=warm_fixed[1][:],
                                        rhs=warm_moving[0][:].bitcast(E4), rhs_scale=warm_moving[1][:],
                                        start=True, stop=True)

            step("tensor", ("warm", len(queues["tensor"])), [("warm_operands",)], emit)

        def spread(operand):
            interleave("vector", operand)

        step("vector", ("warm_operands",), [], make_warm_operands)
        step("vector", ("gates",), [], make_gates)
        for j in range(2):
            gate(0, 0, j)
            gate(1, 0, j)
        for stream in range(2):
            gate(stream, 0, 2)
            gate(stream, 0, 3)
        for n in range(2):
            spread(("dz", 0, n))
            quantise(("dvt", 0, n))
        for h in range(2):
            quantise(("dz", 0, h))
        for h in range(2):
            quantise(("w", 0, h))
        for j in range(PACK):
            gate(0, 1, j)
        spread(("dz", 1, 0))
        for h in range(2):
            quantise(("w", 1, h))
        quantise(("dz", 2, 0))
        quantise(("dz", 1, 0))
        quantise(("dvt", 1, 0))
        spread(("x", 0, 0))
        quantise(("dvt", 1, 1))
        spread(("x", 0, 1))
        quantise(("x", 0, 0))
        spread(("dz", 1, 1))
        quantise(("x", 0, 1))
        for j in range(PACK):
            gate(1, 1, j)
        quantise(("dz", 1, 1))
        spread(("dz", 3, 0))
        spread(("x", 1, 0))
        quantise(("dz", 3, 0))
        quantise(("x", 1, 0))
        quantise(("x", 1, 1))
        spread(("x", 1, 2))
        quantise(("x", 0, 2))
        quantise(("x", 1, 2))
        spread(("dz", 2, 1))
        quantise(("dz", 2, 1))
        spread(("dz", 3, 1))
        quantise(("x", 0, 3))
        quantise(("dz", 3, 1))
        spread(("x", 1, 3))
        quantise(("x", 1, 3))

        warm_up(WARM_FIRST)
        for pair in range(2):
            turn(("dvt", 0, 0), pair)
        warm_up(WARM_BETWEEN)
        for pair in range(2):
            turn(("dvt", 0, 1), pair)
        for quarter, (ch, rp) in enumerate([(0, 0), (0, 1), (1, 0)]):
            interleave("scalar", ("dz", 2, 0), quarter, QUARTERS)
            warm_up(WARM_BETWEEN)
            for h in range(2):
                turn(("w", ch, h), rp)
        interleave("scalar", ("dz", 2, 0), QUARTERS - 1, QUARTERS)
        free_banks.extend([0, 1])
        multiply(("out0", 0, 0, 0), [0, 1])
        for h in range(2):
            turn(("w", 1, h), 1)
        for jp in range(2):
            multiply(("out0", 0, jp + 1, 0), [0, 1])
            empty_out0(0, jp, 0)
            for pair in range(2):
                turn(("dvt", 1, jp), pair)
        multiply(("out0", 0, 3, 0), [0, 1])
        for j in (2, 3):
            empty_out0(0, j, 0)
        for b, j, ch in [(0, j, 1) for j in range(PACK)] + [(1, j, ch) for j in range(PACK) for ch in range(2)]:
            multiply(("out0", b, j, ch), [0, 1])
            empty_out0(b, j, ch)

        for r in range(4):
            multiply(("out1", r, 0), [0, 1])
        for t in range(2):
            for r in range(4):
                multiply(("out1", r, 1), [t])
        interleave("scalar", ("x", 1, 1))
        interleave("scalar", ("x", 0, 2))
        for r in range(4):
            multiply(("out1", r, 0), [2, 3])
            empty_out1(r, 0)
        interleave("scalar", ("x", 0, 3))
        for r in (4, 5):
            multiply(("out1", r, 0), [0, 1])
        for r in (4, 5):
            multiply(("out1", r, 0), [2, 3])
            empty_out1(r, 0)
        for r in (4, 5):
            multiply(("out1", r, 1), [0, 1])
        for r in range(6):
            multiply(("out1", r, 1), [2])
        for r in range(6):
            multiply(("out1", r, 1), [3])
            empty_out1(r, 1, "vector" if r == 5 else "scalar")
        for r in (6, 7):
            multiply(("out1", r, 0), [0, 1])
        multiply(("out1", 6, 1), [0, 1])
        for r in (6, 7):
            multiply(("out1", r, 0), [2, 3])
            empty_out1(r, 0, "vector" if r == 7 else "scalar")
        multiply(("out1", 6, 1), [2, 3])
        empty_out1(6, 1)
        multiply(("out1", 7, 1), [0, 1, 2, 3])
        empty_out1(7, 1, "vector")

        done = set()
        heads = {engine: 0 for engine in queues}
        left = sum(len(steps) for steps in queues.values())
        while left:
            before = left
            for engine, steps in queues.items():
                while heads[engine] < len(steps) and all(need in done for need in steps[heads[engine]][1]):
                    key, needs, emit = steps[heads[engine]]
                    emit()
                    done.add(key)
                    heads[engine] = heads[engine] + 1
                    left = left - 1
            assert left < before
